import numpy as np
import ml_dtypes


def mxq(x, axis, fmt="e4m3"):
    dtype, down = {"e4m3": (ml_dtypes.float8_e4m3fn, 7), "e5m2": (ml_dtypes.float8_e5m2, 14)}[fmt]
    v = np.moveaxis(np.asarray(x, np.float32).astype(ml_dtypes.bfloat16).astype(np.float64), axis, -1)
    blocks = v.reshape(v.shape[:-1] + (-1, 32))
    amax = np.abs(blocks).max(-1, keepdims=True)
    byte = np.maximum(np.where(amax > 0, np.frexp(amax)[1] - 1 + 127, 0) - down, 1)
    scale = np.exp2(byte - 127.0)
    codes = (blocks / scale).astype(np.float32).astype(dtype).astype(np.float64)
    return np.moveaxis((codes * scale).reshape(v.shape), -1, axis)


WIDE = False


def mx_kscale(k):
    if not WIDE:
        return np.ones(k)
    levels = np.array([10, -10, 5, -5, 0])
    a = np.random.permutation(np.resize(levels, k // 512 * 4)).reshape(k // 512, 4)
    idx = np.arange(k)
    return np.exp2(a[idx // 512, idx % 128 // 32])


BF16 = ml_dtypes.bfloat16


def bf(x):
    return np.asarray(x, np.float32).astype(BF16)


def f64(x):
    return np.asarray(x).astype(np.float64)


B, T, D, H, KH, F = 2, 128, 1024, 8, 2, 4096
EPS = 1e-5


def layer_norm(v, g, b):
    m = v.mean(-1, keepdims=True)
    var = ((v - m) ** 2).mean(-1, keepdims=True)
    return (v - m) / np.sqrt(var + EPS) * g + b


def setup_inputs():
    s, t = mx_kscale(D), mx_kscale(D)
    return {
        "h_attn": bf(np.random.standard_normal((B, T, D)) * 0.4 * s),
        "x": bf(np.random.standard_normal((B, T, D))),
        "Wo": bf(np.random.standard_normal((D, D)) * 2.0 / np.sqrt(D) / s[:, None]),
        "bo": bf(np.random.standard_normal(D) * 0.2),
        "ln2_g": bf(1.5 + 0.3 * np.random.standard_normal(D)),
        "ln2_b": bf(0.3 + 0.3 * np.random.standard_normal(D)),
        "fln_g": bf((1.0 + 0.1 * np.random.standard_normal(D)) * t),
        "fln_b": bf(0.2 * np.random.standard_normal(D) * t),
        "W1": bf(np.random.standard_normal((D, F)) / np.sqrt(D) / t[:, None]),
        "b1": bf(np.random.standard_normal(F) * 0.3),
        "W2": bf(np.random.standard_normal((D, F)) / np.sqrt(D) / t[:, None]),
        "b2": bf(np.random.standard_normal(F) * 0.3),
    }


def reference(h_attn, x, Wo, bo, ln2_g, ln2_b, fln_g, fln_b, W1, b1, W2, b2):
    y = f64(x) + ((mxq(f64(h_attn), 2, "e4m3") @ mxq(f64(Wo), 0, "e4m3")) + f64(bo))
    r = layer_norm(y, f64(ln2_g), f64(ln2_b))
    h2q = mxq(layer_norm(r, f64(fln_g), f64(fln_b)), 2, "e4m3")
    g_pre = (h2q @ mxq(f64(W1), 0, "e4m3")) + f64(b1)
    hidden = (h2q @ mxq(f64(W2), 0, "e4m3")) + f64(b2)
    return r, g_pre, hidden

@@ -1,0 +1,232 @@
+from contextlib import ExitStack
+
+import concourse.mybir as mybir
+from concourse.masks import make_identity
+
+F32 = mybir.dt.float32
+BF16 = mybir.dt.bfloat16
+U32 = mybir.dt.uint32
+U8 = mybir.dt.uint8
+FP8X4 = mybir.dt.float8_e4m3fn_x4
+ALU = mybir.AluOpType
+ACT = mybir.ActivationFunctionType
+
+P = 128
+PACK = 4
+K_PASS = P * PACK
+TOKENS = 256
+TOKEN_TILES = TOKENS // P
+D = 1024
+F = 4096
+PASSES = D // K_PASS
+K_BLOCKS = D // P
+BANK = 512
+UNIT_COLS = 1024
+RUN = 4
+VECTOR_COLS = 320
+EPS = 1e-5
+
+FLOPS = 2 * TOKENS * D * (D + 2 * F)
+
+
+def tile_transformerblock_pa_kernel(
+    tc, h_attn, x, Wo, bo, ln2_g, ln2_b, fln_g, fln_b, W1, b1, W2, b2, out_0, out_1, out_2
+):
+    nc = tc.nc
+    r_out = out_0.flatten_outer_dims()
+    g_pre_out = out_1.flatten_outer_dims()
+    hidden_out = out_2.flatten_outer_dims()
+
+    with ExitStack() as ctx:
+        consts = ctx.enter_context(tc.tile_pool(name="consts", bufs=1))
+        small = ctx.enter_context(tc.tile_pool(name="small", bufs=4))
+        rows = ctx.enter_context(tc.tile_pool(name="rows", bufs=5))
+        acts = ctx.enter_context(tc.tile_pool(name="acts", bufs=2))
+        raw_pool = ctx.enter_context(tc.tile_pool(name="raw", bufs=4))
+        grouped_pool = ctx.enter_context(tc.tile_pool(name="grouped", bufs=3))
+        keep = ctx.enter_context(tc.tile_pool(name="keep", bufs=1))
+        staged_pool = ctx.enter_context(tc.tile_pool(name="staged", bufs=4))
+        psum_plain = ctx.enter_context(tc.psum_pool(name="psum_plain", bufs=3))
+        psum_acc = ctx.enter_context(tc.psum_pool(name="psum_acc", bufs=5))
+
+        ident = consts.tile([P, P], BF16)
+        make_identity(nc, ident[:])
+
+        eps = consts.tile([P, 1], F32)
+        nc.vector.memset(eps[:], EPS)
+        table_warmer = consts.tile([P, 1], F32)
+        nc.scalar.activation(out=table_warmer[:], in_=eps[:], func=ACT.Sqrt)
+
+        def load_as_rows(key, vectors):
+            vec_rows = consts.tile([P, BANK], BF16, name="rows_" + key)
+            nc.vector.memset(vec_rows[:], 0.0)
+            first_row = []
+            next_row = 0
+            for vec in vectors:
+                n_rows = vec.shape[0] // BANK
+                nc.sync.dma_start(
+                    out=vec_rows[next_row : next_row + n_rows, :],
+                    in_=vec.rearrange("(r c) -> r c", c=BANK),
+                )
+                first_row.append(next_row)
+                next_row += n_rows
+            return vec_rows, first_row
+
+        norm_rows, norm_first = load_as_rows("norm", (bo, ln2_g, ln2_b, fln_g, fln_b))
+        h_sb = consts.tile([P, TOKEN_TILES, D], BF16)
+        nc.sync.dma_start(
+            out=h_sb[:], in_=h_attn.flatten_outer_dims().rearrange("(m p) d -> p m d", p=P)
+        )
+        x_sb = consts.tile([P, TOKEN_TILES, D], BF16)
+        nc.sync.dma_start(out=x_sb[:], in_=x.flatten_outer_dims().rearrange("(m p) d -> p m d", p=P))
+
+        def spread(key, vec_rows, first_row, width):
+            everywhere = consts.tile([P, width], BF16, name="everywhere_" + key)
+            for pair in range(width // (2 * BANK)):
+                bank = psum_plain.tile([P, 2 * BANK], BF16, tag="plain")
+                for s in range(2):
+                    r = first_row + 2 * pair + s
+                    nc.tensor.matmul(
+                        out=bank[:, s * BANK : (s + 1) * BANK],
+                        lhsT=ident[:, r : r + 1].to_broadcast([P, P]),
+                        rhs=vec_rows[:],
+                        start=True,
+                        stop=True,
+                    )
+                nc.scalar.copy(
+                    out=everywhere[:, pair * 2 * BANK : (pair + 1) * 2 * BANK], in_=bank[:]
+                )
+            return everywhere
+
+        def quantise_tokens(key, token_rows):
+            flipped = psum_plain.tile([P, K_BLOCKS, P], BF16, tag="plain")
+            for kb in range(K_BLOCKS):
+                nc.tensor.transpose(flipped[:, kb, :], token_rows[:, kb * P : (kb + 1) * P], ident[:])
+            grouped = acts.tile([P, PASSES, P, PACK], BF16, tag="token_grouped", align_bytes=64)
+            nc.scalar.copy(
+                out=grouped[:], in_=flipped[:].rearrange("p (g t) r -> p g r t", t=PACK)
+            )
+            codes = keep.tile([P, PASSES * P], U32, name="codes_" + key, align_bytes=64)
+            scales = keep.tile([P, PASSES * P], U8, name="scales_" + key, align_bytes=64)
+            nc.vector.quantize_mx(
+                out=codes[:].bitcast(FP8X4),
+                scales=scales[:],
+                in_=grouped[:].rearrange("p g r t -> p (g r t)"),
+            )
+            return codes, scales
+
+        def quantise_weights(key, w, first_col):
+            unit = []
+            for g in range(PASSES):
+                raw = raw_pool.tile([P, PACK, UNIT_COLS], BF16, tag="raw")
+                nc.sync.dma_start(
+                    out=raw[:],
+                    in_=w[
+                        g * K_PASS : (g + 1) * K_PASS, first_col : first_col + UNIT_COLS
+                    ].rearrange("(t p) n -> p t n", p=P),
+                )
+                grouped = grouped_pool.tile(
+                    [P, UNIT_COLS, PACK], BF16, tag="grouped", align_bytes=64
+                )
+                dst = grouped[:].rearrange("p (c i) t -> p c t i", i=RUN)
+                src = raw[:].rearrange("p t (c i) -> p c t i", i=RUN)
+                split = VECTOR_COLS // RUN
+                nc.vector.tensor_copy(out=dst[:, :split], in_=src[:, :split])
+                nc.scalar.copy(out=dst[:, split:], in_=src[:, split:])
+                codes = keep.tile(
+                    [P, UNIT_COLS], U32, name="codes_%s_%d" % (key, g), align_bytes=64
+                )
+                scales = keep.tile(
+                    [P, UNIT_COLS], U8, name="scales_%s_%d" % (key, g), align_bytes=64
+                )
+                nc.vector.quantize_mx(
+                    out=codes[:].bitcast(FP8X4),
+                    scales=scales[:],
+                    in_=grouped[:].rearrange("p n t -> p (n t)"),
+                )
+                unit.append((codes, scales))
+            return unit
+
+        def product(tokens_q, unit, n):
+            token_codes, token_scales = tokens_q
+            acc = psum_acc.tile([P, BANK], F32, tag="acc")
+            for g in range(PASSES):
+                w_codes, w_scales = unit[g]
+                nc.tensor.matmul_mx(
+                    out=acc[:],
+                    lhsT=token_codes[:, g * P : (g + 1) * P].bitcast(FP8X4),
+                    lhsT_scale=token_scales[:, g * P : (g + 1) * P],
+                    rhs=w_codes[:, n * BANK : (n + 1) * BANK].bitcast(FP8X4),
+                    rhs_scale=w_scales[:, n * BANK : (n + 1) * BANK],
+                    start=(g == 0),
+                    stop=(g == PASSES - 1),
+                )
+            return acc
+
+        def layer_norm(src, gain, bias, scratch, dest):
+            stats = small.tile([P, D // BANK, 6], F32, tag="stats")
+            for s in range(D // BANK):
+                nc.vector.bn_stats(out=stats[:, s, :], in_=src[:, s * BANK : (s + 1) * BANK])
+            mean_var = small.tile([P, 2], F32, tag="mean_var")
+            nc.vector.bn_aggr(out=mean_var[:], in_=stats[:].rearrange("p s d -> p (s d)"))
+            std = small.tile([P, 1], F32, tag="std")
+            nc.scalar.activation(out=std[:], in_=mean_var[:, 1:2], func=ACT.Sqrt, bias=eps[:])
+            rstd = small.tile([P, 1], F32, tag="rstd")
+            nc.vector.reciprocal(out=rstd[:], in_=std[:])
+            nc.vector.scalar_tensor_tensor(
+                out=scratch[:],
+                in0=src[:],
+                scalar=mean_var[:, 0:1],
+                in1=gain[:],
+                op0=ALU.subtract,
+                op1=ALU.mult,
+            )
+            nc.vector.scalar_tensor_tensor(
+                out=dest[:], in0=scratch[:], scalar=rstd[:], in1=bias[:], op0=ALU.mult, op1=ALU.add
+            )
+
+        wo_unit = quantise_weights("wo", Wo, 0)
+        bias_rows, bias_first = load_as_rows("bias", (b1, b2))
+        bo_all = spread("bo", norm_rows, norm_first[0], D)
+        h_q = [quantise_tokens("h%d" % m, h_sb[:, m, :]) for m in range(TOKEN_TILES)]
+        ln2_g_all = spread("ln2_g", norm_rows, norm_first[1], D)
+        ln2_b_all = spread("ln2_b", norm_rows, norm_first[2], D)
+        fln_g_all = spread("fln_g", norm_rows, norm_first[3], D)
+        fln_b_all = spread("fln_b", norm_rows, norm_first[4], D)
+
+        h2_q = []
+        for m in range(TOKEN_TILES):
+            x_plus_bo = rows.tile([P, D], F32, tag="row")
+            nc.vector.tensor_tensor(out=x_plus_bo[:], in0=x_sb[:, m, :], in1=bo_all[:], op=ALU.add)
+            r = rows.tile([P, D], F32, tag="row")
+            for n in range(D // BANK):
+                acc = product(h_q[m], wo_unit, n)
+                cols = slice(n * BANK, (n + 1) * BANK)
+                nc.vector.tensor_tensor(out=r[:, cols], in0=acc[:], in1=x_plus_bo[:, cols], op=ALU.add)
+            layer_norm(r, ln2_g_all, ln2_b_all, r, r)
+            nc.sync.dma_start(out=r_out[m * P : (m + 1) * P, :], in_=r[:])
+            scratch = rows.tile([P, D], F32, tag="row")
+            h2 = acts.tile([P, D], BF16, tag="h2")
+            layer_norm(r, fln_g_all, fln_b_all, scratch, h2)
+            h2_q.append(quantise_tokens("h2_%d" % m, h2))
+
+        bias_all = {
+            "w1": spread("b1", bias_rows, bias_first[0], F),
+            "w2": spread("b2", bias_rows, bias_first[1], F),
+        }
+        for key, w, out in (("w1", W1, g_pre_out), ("w2", W2, hidden_out)):
+            for first_col in range(0, F, UNIT_COLS):
+                unit = quantise_weights("%s_%d" % (key, first_col), w, first_col)
+                for m in range(TOKEN_TILES):
+                    staged = staged_pool.tile([P, UNIT_COLS], F32, tag="staged")
+                    for n in range(UNIT_COLS // BANK):
+                        acc = product(h2_q[m], unit, n)
+                        nc.vector.tensor_tensor(
+                            out=staged[:, n * BANK : (n + 1) * BANK],
+                            in0=acc[:],
+                            in1=bias_all[key][:, first_col + n * BANK : first_col + (n + 1) * BANK],
+                            op=ALU.add,
+                        )
+                    nc.sync.dma_start(
+                        out=out[m * P : (m + 1) * P, first_col : first_col + UNIT_COLS], in_=staged[:]
+                    )

@@ -21,9 +21,14 @@ F = 4096
 PASSES = D // K_PASS
 K_BLOCKS = D // P
 BANK = 512
+PSUM_BANKS = 8
 UNIT_COLS = 1024
+UNIT_BANKS = UNIT_COLS // BANK
+RAW_BUFS = 8
 RUN = 4
-VECTOR_COLS = 320
+TOGETHER_COLS = 672
+STEADY_COLS = 320
+NORM_UNITS = 4
 EPS = 1e-5
 
 FLOPS = 2 * TOKENS * D * (D + 2 * F)
@@ -34,28 +39,30 @@ def tile_transformerblock_pa_kernel(
 ):
     nc = tc.nc
     r_out = out_0.flatten_outer_dims()
-    g_pre_out = out_1.flatten_outer_dims()
-    hidden_out = out_2.flatten_outer_dims()
+
+    units = []
+    for w, width in ((Wo, D), (W1, F), (W2, F)):
+        for first_col in range(0, width, UNIT_COLS):
+            for g in range(PASSES):
+                units.append((w, first_col, g))
+    first_steady_unit = PASSES + NORM_UNITS
 
     with ExitStack() as ctx:
         consts = ctx.enter_context(tc.tile_pool(name="consts", bufs=1))
-        small = ctx.enter_context(tc.tile_pool(name="small", bufs=4))
-        rows = ctx.enter_context(tc.tile_pool(name="rows", bufs=5))
+        small = ctx.enter_context(tc.tile_pool(name="small", bufs=2))
+        rows = ctx.enter_context(tc.tile_pool(name="rows", bufs=4))
         acts = ctx.enter_context(tc.tile_pool(name="acts", bufs=2))
-        raw_pool = ctx.enter_context(tc.tile_pool(name="raw", bufs=4))
-        grouped_pool = ctx.enter_context(tc.tile_pool(name="grouped", bufs=3))
-        keep = ctx.enter_context(tc.tile_pool(name="keep", bufs=1))
+        raw_pool = ctx.enter_context(tc.tile_pool(name="raw", bufs=RAW_BUFS))
+        grouped_pool = ctx.enter_context(tc.tile_pool(name="grouped", bufs=4))
+        quantised = ctx.enter_context(tc.tile_pool(name="quantised", bufs=10))
         staged_pool = ctx.enter_context(tc.tile_pool(name="staged", bufs=4))
-        psum_plain = ctx.enter_context(tc.psum_pool(name="psum_plain", bufs=3))
-        psum_acc = ctx.enter_context(tc.psum_pool(name="psum_acc", bufs=5))
+        psum = ctx.enter_context(tc.psum_pool(name="psum", bufs=PSUM_BANKS))
+        ctx.enter_context(tc.manual_schedule())
 
-        ident = consts.tile([P, P], BF16)
-        make_identity(nc, ident[:])
-
-        eps = consts.tile([P, 1], F32)
-        nc.vector.memset(eps[:], EPS)
-        table_warmer = consts.tile([P, 1], F32)
-        nc.scalar.activation(out=table_warmer[:], in_=eps[:], func=ACT.Sqrt)
+        raw = {}
+        grouped = {}
+        packed = {}
+        banks = {}
 
         def load_as_rows(key, vectors):
             vec_rows = consts.tile([P, BANK], BF16, name="rows_" + key)
@@ -72,18 +79,10 @@ def tile_transformerblock_pa_kernel(
                 next_row += n_rows
             return vec_rows, first_row
 
-        norm_rows, norm_first = load_as_rows("norm", (bo, ln2_g, ln2_b, fln_g, fln_b))
-        h_sb = consts.tile([P, TOKEN_TILES, D], BF16)
-        nc.sync.dma_start(
-            out=h_sb[:], in_=h_attn.flatten_outer_dims().rearrange("(m p) d -> p m d", p=P)
-        )
-        x_sb = consts.tile([P, TOKEN_TILES, D], BF16)
-        nc.sync.dma_start(out=x_sb[:], in_=x.flatten_outer_dims().rearrange("(m p) d -> p m d", p=P))
-
-        def spread(key, vec_rows, first_row, width):
+        def spread(key, vec_rows, first_row, width, copy_out):
             everywhere = consts.tile([P, width], BF16, name="everywhere_" + key)
             for pair in range(width // (2 * BANK)):
-                bank = psum_plain.tile([P, 2 * BANK], BF16, tag="plain")
+                bank = psum.tile([P, 2 * BANK], BF16, tag="bank")
                 for s in range(2):
                     r = first_row + 2 * pair + s
                     nc.tensor.matmul(
@@ -93,140 +92,208 @@ def tile_transformerblock_pa_kernel(
                         start=True,
                         stop=True,
                     )
-                nc.scalar.copy(
-                    out=everywhere[:, pair * 2 * BANK : (pair + 1) * 2 * BANK], in_=bank[:]
-                )
+                copy_out(out=everywhere[:, pair * 2 * BANK : (pair + 1) * 2 * BANK], in_=bank[:])
             return everywhere
 
-        def quantise_tokens(key, token_rows):
-            flipped = psum_plain.tile([P, K_BLOCKS, P], BF16, tag="plain")
+        def flip_tokens(token_rows):
+            flipped = psum.tile([P, K_BLOCKS, P], BF16, tag="bank")
             for kb in range(K_BLOCKS):
                 nc.tensor.transpose(flipped[:, kb, :], token_rows[:, kb * P : (kb + 1) * P], ident[:])
-            grouped = acts.tile([P, PASSES, P, PACK], BF16, tag="token_grouped", align_bytes=64)
+            token_grouped = acts.tile([P, PASSES, P, PACK], BF16, tag="token_grouped", align_bytes=64)
             nc.scalar.copy(
-                out=grouped[:], in_=flipped[:].rearrange("p (g t) r -> p g r t", t=PACK)
+                out=token_grouped[:], in_=flipped[:].rearrange("p (g t) r -> p g r t", t=PACK)
             )
-            codes = keep.tile([P, PASSES * P], U32, name="codes_" + key, align_bytes=64)
-            scales = keep.tile([P, PASSES * P], U8, name="scales_" + key, align_bytes=64)
+            return token_grouped
+
+        def quantise_tokens(key, token_grouped):
+            codes = consts.tile([P, PASSES * P], U32, name="codes_" + key, align_bytes=64)
+            scales = consts.tile([P, PASSES * P], U8, name="scales_" + key, align_bytes=64)
             nc.vector.quantize_mx(
                 out=codes[:].bitcast(FP8X4),
                 scales=scales[:],
-                in_=grouped[:].rearrange("p g r t -> p (g r t)"),
+                in_=token_grouped[:].rearrange("p g r t -> p (g r t)"),
             )
             return codes, scales
 
-        def quantise_weights(key, w, first_col):
-            unit = []
-            for g in range(PASSES):
-                raw = raw_pool.tile([P, PACK, UNIT_COLS], BF16, tag="raw")
-                nc.sync.dma_start(
-                    out=raw[:],
-                    in_=w[
-                        g * K_PASS : (g + 1) * K_PASS, first_col : first_col + UNIT_COLS
-                    ].rearrange("(t p) n -> p t n", p=P),
-                )
-                grouped = grouped_pool.tile(
-                    [P, UNIT_COLS, PACK], BF16, tag="grouped", align_bytes=64
-                )
-                dst = grouped[:].rearrange("p (c i) t -> p c t i", i=RUN)
-                src = raw[:].rearrange("p t (c i) -> p c t i", i=RUN)
-                split = VECTOR_COLS // RUN
+        def load(u):
+            w, first_col, g = units[u]
+            rows_of_unit = raw_pool.tile([P, PACK, UNIT_COLS], BF16, tag="raw")
+            nc.sync.dma_start(
+                out=rows_of_unit[:],
+                in_=w[g * K_PASS : (g + 1) * K_PASS, first_col : first_col + UNIT_COLS].rearrange(
+                    "(t p) n -> p t n", p=P
+                ),
+            )
+            raw[u] = rows_of_unit
+
+        def regroup(u, vector_cols):
+            side_by_side = grouped_pool.tile([P, UNIT_COLS, PACK], BF16, tag="grouped", align_bytes=64)
+            dst = side_by_side[:].rearrange("p (c i) t -> p c t i", i=RUN)
+            src = raw[u][:].rearrange("p t (c i) -> p c t i", i=RUN)
+            split = vector_cols // RUN
+            if split > 0:
                 nc.vector.tensor_copy(out=dst[:, :split], in_=src[:, :split])
-                nc.scalar.copy(out=dst[:, split:], in_=src[:, split:])
-                codes = keep.tile(
-                    [P, UNIT_COLS], U32, name="codes_%s_%d" % (key, g), align_bytes=64
-                )
-                scales = keep.tile(
-                    [P, UNIT_COLS], U8, name="scales_%s_%d" % (key, g), align_bytes=64
-                )
-                nc.vector.quantize_mx(
-                    out=codes[:].bitcast(FP8X4),
-                    scales=scales[:],
-                    in_=grouped[:].rearrange("p n t -> p (n t)"),
-                )
-                unit.append((codes, scales))
-            return unit
+            nc.scalar.copy(out=dst[:, split:], in_=src[:, split:])
+            grouped[u] = side_by_side
+            if u + RAW_BUFS < len(units):
+                load(u + RAW_BUFS)
 
-        def product(tokens_q, unit, n):
-            token_codes, token_scales = tokens_q
-            acc = psum_acc.tile([P, BANK], F32, tag="acc")
-            for g in range(PASSES):
-                w_codes, w_scales = unit[g]
-                nc.tensor.matmul_mx(
-                    out=acc[:],
-                    lhsT=token_codes[:, g * P : (g + 1) * P].bitcast(FP8X4),
-                    lhsT_scale=token_scales[:, g * P : (g + 1) * P],
-                    rhs=w_codes[:, n * BANK : (n + 1) * BANK].bitcast(FP8X4),
-                    rhs_scale=w_scales[:, n * BANK : (n + 1) * BANK],
-                    start=(g == 0),
-                    stop=(g == PASSES - 1),
-                )
-            return acc
-
-        def layer_norm(src, gain, bias, scratch, dest):
-            stats = small.tile([P, D // BANK, 6], F32, tag="stats")
-            for s in range(D // BANK):
-                nc.vector.bn_stats(out=stats[:, s, :], in_=src[:, s * BANK : (s + 1) * BANK])
-            mean_var = small.tile([P, 2], F32, tag="mean_var")
-            nc.vector.bn_aggr(out=mean_var[:], in_=stats[:].rearrange("p s d -> p (s d)"))
-            std = small.tile([P, 1], F32, tag="std")
-            nc.scalar.activation(out=std[:], in_=mean_var[:, 1:2], func=ACT.Sqrt, bias=eps[:])
-            rstd = small.tile([P, 1], F32, tag="rstd")
-            nc.vector.reciprocal(out=rstd[:], in_=std[:])
-            nc.vector.scalar_tensor_tensor(
-                out=scratch[:],
-                in0=src[:],
-                scalar=mean_var[:, 0:1],
-                in1=gain[:],
-                op0=ALU.subtract,
-                op1=ALU.mult,
+        def quantise(u):
+            codes = quantised.tile([P, UNIT_COLS], U32, tag="codes", align_bytes=64)
+            scales = quantised.tile([P, UNIT_COLS], U8, tag="scales", align_bytes=64)
+            nc.vector.quantize_mx(
+                out=codes[:].bitcast(FP8X4),
+                scales=scales[:],
+                in_=grouped[u][:].rearrange("p n t -> p (n t)"),
             )
-            nc.vector.scalar_tensor_tensor(
-                out=dest[:], in0=scratch[:], scalar=rstd[:], in1=bias[:], op0=ALU.mult, op1=ALU.add
-            )
+            packed[u] = (codes, scales)
 
-        wo_unit = quantise_weights("wo", Wo, 0)
-        bias_rows, bias_first = load_as_rows("bias", (b1, b2))
-        bo_all = spread("bo", norm_rows, norm_first[0], D)
-        h_q = [quantise_tokens("h%d" % m, h_sb[:, m, :]) for m in range(TOKEN_TILES)]
-        ln2_g_all = spread("ln2_g", norm_rows, norm_first[1], D)
-        ln2_b_all = spread("ln2_b", norm_rows, norm_first[2], D)
-        fln_g_all = spread("fln_g", norm_rows, norm_first[3], D)
-        fln_b_all = spread("fln_b", norm_rows, norm_first[4], D)
-
-        h2_q = []
-        for m in range(TOKEN_TILES):
-            x_plus_bo = rows.tile([P, D], F32, tag="row")
-            nc.vector.tensor_tensor(out=x_plus_bo[:], in0=x_sb[:, m, :], in1=bo_all[:], op=ALU.add)
-            r = rows.tile([P, D], F32, tag="row")
-            for n in range(D // BANK):
-                acc = product(h_q[m], wo_unit, n)
-                cols = slice(n * BANK, (n + 1) * BANK)
-                nc.vector.tensor_tensor(out=r[:, cols], in0=acc[:], in1=x_plus_bo[:, cols], op=ALU.add)
-            layer_norm(r, ln2_g_all, ln2_b_all, r, r)
-            nc.sync.dma_start(out=r_out[m * P : (m + 1) * P, :], in_=r[:])
-            scratch = rows.tile([P, D], F32, tag="row")
-            h2 = acts.tile([P, D], BF16, tag="h2")
-            layer_norm(r, fln_g_all, fln_b_all, scratch, h2)
-            h2_q.append(quantise_tokens("h2_%d" % m, h2))
-
-        bias_all = {
-            "w1": spread("b1", bias_rows, bias_first[0], F),
-            "w2": spread("b2", bias_rows, bias_first[1], F),
-        }
-        for key, w, out in (("w1", W1, g_pre_out), ("w2", W2, hidden_out)):
-            for first_col in range(0, F, UNIT_COLS):
-                unit = quantise_weights("%s_%d" % (key, first_col), w, first_col)
-                for m in range(TOKEN_TILES):
-                    staged = staged_pool.tile([P, UNIT_COLS], F32, tag="staged")
-                    for n in range(UNIT_COLS // BANK):
-                        acc = product(h2_q[m], unit, n)
-                        nc.vector.tensor_tensor(
-                            out=staged[:, n * BANK : (n + 1) * BANK],
-                            in0=acc[:],
-                            in1=bias_all[key][:, first_col + n * BANK : first_col + (n + 1) * BANK],
-                            op=ALU.add,
-                        )
-                    nc.sync.dma_start(
-                        out=out[m * P : (m + 1) * P, first_col : first_col + UNIT_COLS], in_=staged[:]
+        def multiply(u, tokens_q):
+            chunk, g = divmod(u, PASSES)
+            w_codes, w_scales = packed[u]
+            for m in range(TOKEN_TILES):
+                token_codes, token_scales = tokens_q[m]
+                for n in range(UNIT_BANKS):
+                    if g == 0:
+                        acc = psum.tile([P, BANK], F32, tag="bank")
+                        banks[(chunk, m, n)] = acc
+                    nc.tensor.matmul_mx(
+                        out=banks[(chunk, m, n)][:],
+                        lhsT=token_codes[:, g * P : (g + 1) * P].bitcast(FP8X4),
+                        lhsT_scale=token_scales[:, g * P : (g + 1) * P],
+                        rhs=w_codes[:, n * BANK : (n + 1) * BANK].bitcast(FP8X4),
+                        rhs_scale=w_scales[:, n * BANK : (n + 1) * BANK],
+                        start=(g == 0),
+                        stop=(g == PASSES - 1),
                     )
+
+        def add_to_banks(chunk, m, addend, dest):
+            for n in range(UNIT_BANKS):
+                cols = slice(n * BANK, (n + 1) * BANK)
+                nc.vector.tensor_tensor(
+                    out=dest[:, cols], in0=banks[(chunk, m, n)][:], in1=addend[:, cols], op=ALU.add
+                )
+
+        def measure(stats, m, src):
+            for s in range(D // BANK):
+                nc.vector.bn_stats(out=stats[:, m, s, :], in_=src[:, s * BANK : (s + 1) * BANK])
+
+        def mean_and_rstd(stats):
+            mean_var = small.tile([P, TOKEN_TILES, 2], F32, tag="mean_var")
+            for m in range(TOKEN_TILES):
+                nc.vector.bn_aggr(out=mean_var[:, m, :], in_=stats[:, m].rearrange("p s d -> p (s d)"))
+            var_eps = small.tile([P, TOKEN_TILES, 1], F32, tag="var_eps")
+            nc.gpsimd.tensor_scalar(
+                out=var_eps[:], in0=mean_var[:, :, 1:2], scalar1=EPS, scalar2=None, op0=ALU.add
+            )
+            rstd = small.tile([P, TOKEN_TILES, 1], F32, tag="rstd")
+            nc.gpsimd.tensor_tensor(out=rstd[:], in0=var_eps[:], in1=minus_half[:], op=ALU.pow)
+            return mean_var, rstd
+
+        def centre_times_gain(dest, src, mean, gain):
+            nc.vector.scalar_tensor_tensor(
+                out=dest[:], in0=src[:], scalar=mean, in1=gain[:], op0=ALU.subtract, op1=ALU.mult
+            )
+
+        def times_rstd_plus_bias(dest, src, rstd, bias):
+            nc.vector.scalar_tensor_tensor(
+                out=dest[:], in0=src[:], scalar=rstd, in1=bias[:], op0=ALU.mult, op1=ALU.add
+            )
+
+        ident = consts.tile([P, P], BF16)
+        make_identity(nc, ident[:])
+        minus_half = consts.tile([P, TOKEN_TILES, 1], F32)
+        nc.vector.memset(minus_half[:], -0.5)
+
+        norm_rows, norm_first = load_as_rows("norm", (bo, ln2_g, ln2_b, fln_g, fln_b))
+        h_sb = consts.tile([P, TOKEN_TILES, D], BF16)
+        nc.sync.dma_start(
+            out=h_sb[:], in_=h_attn.flatten_outer_dims().rearrange("(m p) d -> p m d", p=P)
+        )
+        x_sb = consts.tile([P, TOKEN_TILES, D], BF16)
+        nc.sync.dma_start(out=x_sb[:], in_=x.flatten_outer_dims().rearrange("(m p) d -> p m d", p=P))
+        for u in range(PASSES):
+            load(u)
+        bias_rows, bias_first = load_as_rows("bias", (b1, b2))
+        for u in range(PASSES, RAW_BUFS):
+            load(u)
+
+        bo_all = spread("bo", norm_rows, norm_first[0], D, nc.vector.tensor_copy)
+        x_plus_bo = []
+        for m in range(TOKEN_TILES):
+            sum_row = rows.tile([P, D], F32, tag="row")
+            nc.vector.tensor_tensor(out=sum_row[:], in0=x_sb[:, m, :], in1=bo_all[:], op=ALU.add)
+            x_plus_bo.append(sum_row)
+        h_grouped = [flip_tokens(h_sb[:, m, :]) for m in range(TOKEN_TILES)]
+        h_q = [quantise_tokens("h%d" % m, h_grouped[m]) for m in range(TOKEN_TILES)]
+        ln2_g_all = spread("ln2_g", norm_rows, norm_first[1], D, nc.scalar.copy)
+        regroup(0, TOGETHER_COLS)
+        ln2_b_all = spread("ln2_b", norm_rows, norm_first[2], D, nc.scalar.copy)
+        quantise(0)
+        multiply(0, h_q)
+        regroup(1, TOGETHER_COLS)
+        fln_g_all = spread("fln_g", norm_rows, norm_first[3], D, nc.scalar.copy)
+        fln_b_all = spread("fln_b", norm_rows, norm_first[4], D, nc.scalar.copy)
+        quantise(1)
+        multiply(1, h_q)
+
+        regroup(2, 0)
+        r = []
+        stats = small.tile([P, TOKEN_TILES, D // BANK, 6], F32, tag="stats")
+        for m in range(TOKEN_TILES):
+            r_row = rows.tile([P, D], F32, tag="row")
+            add_to_banks(0, m, x_plus_bo[m], r_row)
+            measure(stats, m, r_row)
+            r.append(r_row)
+        mean_var, rstd = mean_and_rstd(stats)
+        b1_all = spread("b1", bias_rows, bias_first[0], F, nc.scalar.copy)
+        for m in range(TOKEN_TILES):
+            centre_times_gain(r[m], r[m], mean_var[:, m, 0:1], ln2_g_all)
+        regroup(3, 0)
+        quantise(2)
+        stats = small.tile([P, TOKEN_TILES, D // BANK, 6], F32, tag="stats")
+        for m in range(TOKEN_TILES):
+            times_rstd_plus_bias(r[m], r[m], rstd[:, m, :], ln2_b_all)
+            nc.sync.dma_start(out=r_out[m * P : (m + 1) * P, :], in_=r[m][:])
+            measure(stats, m, r[m])
+        mean_var, rstd = mean_and_rstd(stats)
+        b2_all = spread("b2", bias_rows, bias_first[1], F, nc.scalar.copy)
+        centred = []
+        for m in range(TOKEN_TILES):
+            centred_row = rows.tile([P, D], F32, tag="row")
+            centre_times_gain(centred_row, r[m], mean_var[:, m, 0:1], fln_g_all)
+            centred.append(centred_row)
+        regroup(4, 0)
+        quantise(3)
+        h2_grouped = []
+        for m in range(TOKEN_TILES):
+            h2 = acts.tile([P, D], BF16, tag="h2")
+            times_rstd_plus_bias(h2, centred[m], rstd[:, m, :], fln_b_all)
+            h2_grouped.append(flip_tokens(h2))
+        regroup(5, 0)
+        quantise(4)
+        h2_q = [quantise_tokens("h2_%d" % m, h2_grouped[m]) for m in range(TOKEN_TILES)]
+
+        def finish(chunk, m):
+            w, first_col, g = units[chunk * PASSES]
+            out, bias = (out_1, b1_all) if w is W1 else (out_2, b2_all)
+            staged = staged_pool.tile([P, UNIT_COLS], F32, tag="staged")
+            add_to_banks(chunk, m, bias[:, first_col : first_col + UNIT_COLS], staged)
+            nc.sync.dma_start(
+                out=out.flatten_outer_dims()[m * P : (m + 1) * P, first_col : first_col + UNIT_COLS],
+                in_=staged[:],
+            )
+
+        for u in range(PASSES, first_steady_unit - 1):
+            multiply(u, h2_q)
+        for m in range(TOKEN_TILES):
+            finish(1, m)
+        for u in range(first_steady_unit, len(units)):
+            quantise(u - 1)
+            multiply(u - 1, h2_q)
+            regroup(u, STEADY_COLS)
+            finish((u - PASSES) // PASSES, u % TOKEN_TILES)
+        quantise(len(units) - 1)
+        multiply(len(units) - 1, h2_q)
+        for m in range(TOKEN_TILES):
+            finish(len(units) // PASSES - 1, m)

@@ -27,8 +27,8 @@ UNIT_BANKS = UNIT_COLS // BANK
 RAW_BUFS = 8
 RUN = 4
 TOGETHER_COLS = 672
-STEADY_COLS = 320
-NORM_UNITS = 4
+STEADY_COLS = 256
+LAG = 2
 EPS = 1e-5
 
 FLOPS = 2 * TOKENS * D * (D + 2 * F)
@@ -45,7 +45,7 @@ def tile_transformerblock_pa_kernel(
         for first_col in range(0, width, UNIT_COLS):
             for g in range(PASSES):
                 units.append((w, first_col, g))
-    first_steady_unit = PASSES + NORM_UNITS
+    last_chunk = len(units) // PASSES - 1
 
     with ExitStack() as ctx:
         consts = ctx.enter_context(tc.tile_pool(name="consts", bufs=1))
@@ -54,7 +54,7 @@ def tile_transformerblock_pa_kernel(
         acts = ctx.enter_context(tc.tile_pool(name="acts", bufs=2))
         raw_pool = ctx.enter_context(tc.tile_pool(name="raw", bufs=RAW_BUFS))
         grouped_pool = ctx.enter_context(tc.tile_pool(name="grouped", bufs=4))
-        quantised = ctx.enter_context(tc.tile_pool(name="quantised", bufs=10))
+        quantised = ctx.enter_context(tc.tile_pool(name="quantised", bufs=6))
         staged_pool = ctx.enter_context(tc.tile_pool(name="staged", bufs=4))
         psum = ctx.enter_context(tc.psum_pool(name="psum", bufs=PSUM_BANKS))
         ctx.enter_context(tc.manual_schedule())
@@ -133,7 +133,8 @@ def tile_transformerblock_pa_kernel(
             split = vector_cols // RUN
             if split > 0:
                 nc.vector.tensor_copy(out=dst[:, :split], in_=src[:, :split])
-            nc.scalar.copy(out=dst[:, split:], in_=src[:, split:])
+            if split < UNIT_COLS // RUN:
+                nc.scalar.copy(out=dst[:, split:], in_=src[:, split:])
             grouped[u] = side_by_side
             if u + RAW_BUFS < len(units):
                 load(u + RAW_BUFS)
@@ -167,37 +168,42 @@ def tile_transformerblock_pa_kernel(
                         stop=(g == PASSES - 1),
                     )
 
-        def add_to_banks(chunk, m, addend, dest):
-            for n in range(UNIT_BANKS):
-                cols = slice(n * BANK, (n + 1) * BANK)
-                nc.vector.tensor_tensor(
-                    out=dest[:, cols], in0=banks[(chunk, m, n)][:], in1=addend[:, cols], op=ALU.add
-                )
+        def new_statistics():
+            half_sums = small.tile([P, TOKEN_TILES, UNIT_BANKS], F32, tag="half_sums")
+            minus_mean = small.tile([P, TOKEN_TILES, 1], F32, tag="minus_mean")
+            sum_sq = small.tile([P, TOKEN_TILES, 1], F32, tag="sum_sq")
+            return half_sums, minus_mean, sum_sq
 
-        def measure(stats, m, src):
-            for s in range(D // BANK):
-                nc.vector.bn_stats(out=stats[:, m, s, :], in_=src[:, s * BANK : (s + 1) * BANK])
+        def measure(m, src, half_sums, minus_mean, sum_sq):
+            nc.vector.tensor_scalar(
+                out=minus_mean[:, m, :],
+                in0=half_sums[:, m, 0:1],
+                scalar1=half_sums[:, m, 1:2],
+                scalar2=-1.0 / D,
+                op0=ALU.add,
+                op1=ALU.mult,
+            )
+            squares = acts.tile([P, D], BF16, tag="squares")
+            nc.scalar.activation(
+                out=squares[:],
+                in_=src[:],
+                func=ACT.Square,
+                bias=minus_mean[:, m, :],
+                accum_out=sum_sq[:, m, :],
+            )
 
-        def mean_and_rstd(stats):
-            mean_var = small.tile([P, TOKEN_TILES, 2], F32, tag="mean_var")
-            for m in range(TOKEN_TILES):
-                nc.vector.bn_aggr(out=mean_var[:, m, :], in_=stats[:, m].rearrange("p s d -> p (s d)"))
+        def rstd_of(sum_sq):
             var_eps = small.tile([P, TOKEN_TILES, 1], F32, tag="var_eps")
             nc.gpsimd.tensor_scalar(
-                out=var_eps[:], in0=mean_var[:, :, 1:2], scalar1=EPS, scalar2=None, op0=ALU.add
+                out=var_eps[:], in0=sum_sq[:], scalar1=1.0 / D, scalar2=EPS, op0=ALU.mult, op1=ALU.add
             )
             rstd = small.tile([P, TOKEN_TILES, 1], F32, tag="rstd")
             nc.gpsimd.tensor_tensor(out=rstd[:], in0=var_eps[:], in1=minus_half[:], op=ALU.pow)
-            return mean_var, rstd
+            return rstd
 
-        def centre_times_gain(dest, src, mean, gain):
+        def centre_times_gain(dest, src, minus_mean, gain):
             nc.vector.scalar_tensor_tensor(
-                out=dest[:], in0=src[:], scalar=mean, in1=gain[:], op0=ALU.subtract, op1=ALU.mult
-            )
-
-        def times_rstd_plus_bias(dest, src, rstd, bias):
-            nc.vector.scalar_tensor_tensor(
-                out=dest[:], in0=src[:], scalar=rstd, in1=bias[:], op0=ALU.mult, op1=ALU.add
+                out=dest[:], in0=src[:], scalar=minus_mean, in1=gain[:], op0=ALU.add, op1=ALU.mult
             )
 
         ident = consts.tile([P, P], BF16)
@@ -232,68 +238,97 @@ def tile_transformerblock_pa_kernel(
         quantise(0)
         multiply(0, h_q)
         regroup(1, TOGETHER_COLS)
-        fln_g_all = spread("fln_g", norm_rows, norm_first[3], D, nc.scalar.copy)
-        fln_b_all = spread("fln_b", norm_rows, norm_first[4], D, nc.scalar.copy)
         quantise(1)
         multiply(1, h_q)
 
         regroup(2, 0)
+        half_sums, minus_mean, sum_sq = new_statistics()
         r = []
-        stats = small.tile([P, TOKEN_TILES, D // BANK, 6], F32, tag="stats")
         for m in range(TOKEN_TILES):
             r_row = rows.tile([P, D], F32, tag="row")
-            add_to_banks(0, m, x_plus_bo[m], r_row)
-            measure(stats, m, r_row)
+            for n in range(UNIT_BANKS):
+                cols = slice(n * BANK, (n + 1) * BANK)
+                nc.vector.scalar_tensor_tensor(
+                    out=r_row[:, cols],
+                    in0=banks[(0, m, n)][:],
+                    scalar=1.0,
+                    in1=x_plus_bo[m][:, cols],
+                    op0=ALU.mult,
+                    op1=ALU.add,
+                    accum_out=half_sums[:, m, n : n + 1],
+                )
+            measure(m, r_row, half_sums, minus_mean, sum_sq)
             r.append(r_row)
-        mean_var, rstd = mean_and_rstd(stats)
-        b1_all = spread("b1", bias_rows, bias_first[0], F, nc.scalar.copy)
+        rstd = rstd_of(sum_sq)
+        fln_g_all = spread("fln_g", norm_rows, norm_first[3], D, nc.scalar.copy)
+        fln_b_all = spread("fln_b", norm_rows, norm_first[4], D, nc.scalar.copy)
         for m in range(TOKEN_TILES):
-            centre_times_gain(r[m], r[m], mean_var[:, m, 0:1], ln2_g_all)
-        regroup(3, 0)
+            centre_times_gain(r[m], r[m], minus_mean[:, m, :], ln2_g_all)
         quantise(2)
-        stats = small.tile([P, TOKEN_TILES, D // BANK, 6], F32, tag="stats")
+        b1_all = spread("b1", bias_rows, bias_first[0], F, nc.scalar.copy)
+        half_sums, minus_mean, sum_sq = new_statistics()
         for m in range(TOKEN_TILES):
-            times_rstd_plus_bias(r[m], r[m], rstd[:, m, :], ln2_b_all)
+            for n in range(UNIT_BANKS):
+                cols = slice(n * BANK, (n + 1) * BANK)
+                nc.vector.scalar_tensor_tensor(
+                    out=r[m][:, cols],
+                    in0=r[m][:, cols],
+                    scalar=rstd[:, m, :],
+                    in1=ln2_b_all[:, cols],
+                    op0=ALU.mult,
+                    op1=ALU.add,
+                    accum_out=half_sums[:, m, n : n + 1],
+                )
             nc.sync.dma_start(out=r_out[m * P : (m + 1) * P, :], in_=r[m][:])
-            measure(stats, m, r[m])
-        mean_var, rstd = mean_and_rstd(stats)
-        b2_all = spread("b2", bias_rows, bias_first[1], F, nc.scalar.copy)
+            measure(m, r[m], half_sums, minus_mean, sum_sq)
+        rstd = rstd_of(sum_sq)
         centred = []
         for m in range(TOKEN_TILES):
             centred_row = rows.tile([P, D], F32, tag="row")
-            centre_times_gain(centred_row, r[m], mean_var[:, m, 0:1], fln_g_all)
+            centre_times_gain(centred_row, r[m], minus_mean[:, m, :], fln_g_all)
             centred.append(centred_row)
-        regroup(4, 0)
-        quantise(3)
+        regroup(3, 0)
         h2_grouped = []
         for m in range(TOKEN_TILES):
             h2 = acts.tile([P, D], BF16, tag="h2")
-            times_rstd_plus_bias(h2, centred[m], rstd[:, m, :], fln_b_all)
+            nc.vector.scalar_tensor_tensor(
+                out=h2[:],
+                in0=centred[m][:],
+                scalar=rstd[:, m, :],
+                in1=fln_b_all[:],
+                op0=ALU.mult,
+                op1=ALU.add,
+            )
             h2_grouped.append(flip_tokens(h2))
-        regroup(5, 0)
-        quantise(4)
+        b2_all = spread("b2", bias_rows, bias_first[1], F, nc.scalar.copy)
+        regroup(4, UNIT_COLS)
+        regroup(5, UNIT_COLS)
+        quantise(3)
         h2_q = [quantise_tokens("h2_%d" % m, h2_grouped[m]) for m in range(TOKEN_TILES)]
 
         def finish(chunk, m):
             w, first_col, g = units[chunk * PASSES]
             out, bias = (out_1, b1_all) if w is W1 else (out_2, b2_all)
             staged = staged_pool.tile([P, UNIT_COLS], F32, tag="staged")
-            add_to_banks(chunk, m, bias[:, first_col : first_col + UNIT_COLS], staged)
+            for n in range(UNIT_BANKS):
+                nc.vector.tensor_tensor(
+                    out=staged[:, n * BANK : (n + 1) * BANK],
+                    in0=banks[(chunk, m, n)][:],
+                    in1=bias[:, first_col + n * BANK : first_col + (n + 1) * BANK],
+                    op=ALU.add,
+                )
             nc.sync.dma_start(
                 out=out.flatten_outer_dims()[m * P : (m + 1) * P, first_col : first_col + UNIT_COLS],
                 in_=staged[:],
             )
 
-        for u in range(PASSES, first_steady_unit - 1):
+        for u in range(PASSES, 2 * PASSES):
             multiply(u, h2_q)
+        for u in range(3 * PASSES, len(units) + LAG):
+            quantise(u - LAG)
+            multiply(u - LAG, h2_q)
+            if u < len(units):
+                regroup(u, STEADY_COLS)
+            finish((u - LAG - PASSES) // PASSES, u % TOKEN_TILES)
         for m in range(TOKEN_TILES):
-            finish(1, m)
-        for u in range(first_steady_unit, len(units)):
-            quantise(u - 1)
-            multiply(u - 1, h2_q)
-            regroup(u, STEADY_COLS)
-            finish((u - PASSES) // PASSES, u % TOKEN_TILES)
-        quantise(len(units) - 1)
-        multiply(len(units) - 1, h2_q)
-        for m in range(TOKEN_TILES):
-            finish(len(units) // PASSES - 1, m)
+            finish(last_chunk, m)

@@ -57,7 +57,6 @@ def tile_transformerblock_pa_kernel(
         quantised = ctx.enter_context(tc.tile_pool(name="quantised", bufs=6))
         staged_pool = ctx.enter_context(tc.tile_pool(name="staged", bufs=4))
         psum = ctx.enter_context(tc.psum_pool(name="psum", bufs=PSUM_BANKS))
-        ctx.enter_context(tc.manual_schedule())
 
         raw = {}
         grouped = {}

from contextlib import ExitStack

import concourse.mybir as mybir
from concourse.masks import make_identity

F32 = mybir.dt.float32
BF16 = mybir.dt.bfloat16
U32 = mybir.dt.uint32
U8 = mybir.dt.uint8
FP8X4 = mybir.dt.float8_e4m3fn_x4
ALU = mybir.AluOpType
ACT = mybir.ActivationFunctionType

P = 128
PACK = 4
K_PASS = P * PACK
TOKENS = 256
TOKEN_TILES = TOKENS // P
D = 1024
F = 4096
PASSES = D // K_PASS
K_BLOCKS = D // P
BANK = 512
PSUM_BANKS = 8
UNIT_COLS = 1024
UNIT_BANKS = UNIT_COLS // BANK
RAW_BUFS = 8
RUN = 4
TOGETHER_COLS = 672
STEADY_COLS = 256
LAG = 2
EPS = 1e-5

FLOPS = 2 * TOKENS * D * (D + 2 * F)


def tile_transformerblock_pa_kernel(
    tc, h_attn, x, Wo, bo, ln2_g, ln2_b, fln_g, fln_b, W1, b1, W2, b2, out_0, out_1, out_2
):
    nc = tc.nc
    r_out = out_0.flatten_outer_dims()

    units = []
    for w, width in ((Wo, D), (W1, F), (W2, F)):
        for first_col in range(0, width, UNIT_COLS):
            for g in range(PASSES):
                units.append((w, first_col, g))
    last_chunk = len(units) // PASSES - 1

    with ExitStack() as ctx:
        consts = ctx.enter_context(tc.tile_pool(name="consts", bufs=1))
        small = ctx.enter_context(tc.tile_pool(name="small", bufs=2))
        rows = ctx.enter_context(tc.tile_pool(name="rows", bufs=4))
        acts = ctx.enter_context(tc.tile_pool(name="acts", bufs=2))
        raw_pool = ctx.enter_context(tc.tile_pool(name="raw", bufs=RAW_BUFS))
        grouped_pool = ctx.enter_context(tc.tile_pool(name="grouped", bufs=4))
        quantised = ctx.enter_context(tc.tile_pool(name="quantised", bufs=6))
        staged_pool = ctx.enter_context(tc.tile_pool(name="staged", bufs=4))
        psum = ctx.enter_context(tc.psum_pool(name="psum", bufs=PSUM_BANKS))

        raw = {}
        grouped = {}
        packed = {}
        banks = {}

        def load_as_rows(key, vectors):
            vec_rows = consts.tile([P, BANK], BF16, name="rows_" + key)
            nc.vector.memset(vec_rows[:], 0.0)
            first_row = []
            next_row = 0
            for vec in vectors:
                n_rows = vec.shape[0] // BANK
                nc.sync.dma_start(
                    out=vec_rows[next_row : next_row + n_rows, :],
                    in_=vec.rearrange("(r c) -> r c", c=BANK),
                )
                first_row.append(next_row)
                next_row += n_rows
            return vec_rows, first_row

        def spread(key, vec_rows, first_row, width, copy_out):
            everywhere = consts.tile([P, width], BF16, name="everywhere_" + key)
            for pair in range(width // (2 * BANK)):
                bank = psum.tile([P, 2 * BANK], BF16, tag="bank")
                for s in range(2):
                    r = first_row + 2 * pair + s
                    nc.tensor.matmul(
                        out=bank[:, s * BANK : (s + 1) * BANK],
                        lhsT=ident[:, r : r + 1].to_broadcast([P, P]),
                        rhs=vec_rows[:],
                        start=True,
                        stop=True,
                    )
                copy_out(out=everywhere[:, pair * 2 * BANK : (pair + 1) * 2 * BANK], in_=bank[:])
            return everywhere

        def flip_tokens(token_rows):
            flipped = psum.tile([P, K_BLOCKS, P], BF16, tag="bank")
            for kb in range(K_BLOCKS):
                nc.tensor.transpose(flipped[:, kb, :], token_rows[:, kb * P : (kb + 1) * P], ident[:])
            token_grouped = acts.tile([P, PASSES, P, PACK], BF16, tag="token_grouped", align_bytes=64)
            nc.scalar.copy(
                out=token_grouped[:], in_=flipped[:].rearrange("p (g t) r -> p g r t", t=PACK)
            )
            return token_grouped

        def quantise_tokens(key, token_grouped):
            codes = consts.tile([P, PASSES * P], U32, name="codes_" + key, align_bytes=64)
            scales = consts.tile([P, PASSES * P], U8, name="scales_" + key, align_bytes=64)
            nc.vector.quantize_mx(
                out=codes[:].bitcast(FP8X4),
                scales=scales[:],
                in_=token_grouped[:].rearrange("p g r t -> p (g r t)"),
            )
            return codes, scales

        def load(u):
            w, first_col, g = units[u]
            rows_of_unit = raw_pool.tile([P, PACK, UNIT_COLS], BF16, tag="raw")
            nc.sync.dma_start(
                out=rows_of_unit[:],
                in_=w[g * K_PASS : (g + 1) * K_PASS, first_col : first_col + UNIT_COLS].rearrange(
                    "(t p) n -> p t n", p=P
                ),
            )
            raw[u] = rows_of_unit

        def regroup(u, vector_cols):
            side_by_side = grouped_pool.tile([P, UNIT_COLS, PACK], BF16, tag="grouped", align_bytes=64)
            dst = side_by_side[:].rearrange("p (c i) t -> p c t i", i=RUN)
            src = raw[u][:].rearrange("p t (c i) -> p c t i", i=RUN)
            split = vector_cols // RUN
            if split > 0:
                nc.vector.tensor_copy(out=dst[:, :split], in_=src[:, :split])
            if split < UNIT_COLS // RUN:
                nc.scalar.copy(out=dst[:, split:], in_=src[:, split:])
            grouped[u] = side_by_side
            if u + RAW_BUFS < len(units):
                load(u + RAW_BUFS)

        def quantise(u):
            codes = quantised.tile([P, UNIT_COLS], U32, tag="codes", align_bytes=64)
            scales = quantised.tile([P, UNIT_COLS], U8, tag="scales", align_bytes=64)
            nc.vector.quantize_mx(
                out=codes[:].bitcast(FP8X4),
                scales=scales[:],
                in_=grouped[u][:].rearrange("p n t -> p (n t)"),
            )
            packed[u] = (codes, scales)

        def multiply(u, tokens_q):
            chunk, g = divmod(u, PASSES)
            w_codes, w_scales = packed[u]
            for m in range(TOKEN_TILES):
                token_codes, token_scales = tokens_q[m]
                for n in range(UNIT_BANKS):
                    if g == 0:
                        acc = psum.tile([P, BANK], F32, tag="bank")
                        banks[(chunk, m, n)] = acc
                    nc.tensor.matmul_mx(
                        out=banks[(chunk, m, n)][:],
                        lhsT=token_codes[:, g * P : (g + 1) * P].bitcast(FP8X4),
                        lhsT_scale=token_scales[:, g * P : (g + 1) * P],
                        rhs=w_codes[:, n * BANK : (n + 1) * BANK].bitcast(FP8X4),
                        rhs_scale=w_scales[:, n * BANK : (n + 1) * BANK],
                        start=(g == 0),
                        stop=(g == PASSES - 1),
                    )

        def new_statistics():
            half_sums = small.tile([P, TOKEN_TILES, UNIT_BANKS], F32, tag="half_sums")
            minus_mean = small.tile([P, TOKEN_TILES, 1], F32, tag="minus_mean")
            sum_sq = small.tile([P, TOKEN_TILES, 1], F32, tag="sum_sq")
            return half_sums, minus_mean, sum_sq

        def measure(m, src, half_sums, minus_mean, sum_sq):
            nc.vector.tensor_scalar(
                out=minus_mean[:, m, :],
                in0=half_sums[:, m, 0:1],
                scalar1=half_sums[:, m, 1:2],
                scalar2=-1.0 / D,
                op0=ALU.add,
                op1=ALU.mult,
            )
            squares = acts.tile([P, D], BF16, tag="squares")
            nc.scalar.activation(
                out=squares[:],
                in_=src[:],
                func=ACT.Square,
                bias=minus_mean[:, m, :],
                accum_out=sum_sq[:, m, :],
            )

        def rstd_of(sum_sq):
            var_eps = small.tile([P, TOKEN_TILES, 1], F32, tag="var_eps")
            nc.gpsimd.tensor_scalar(
                out=var_eps[:], in0=sum_sq[:], scalar1=1.0 / D, scalar2=EPS, op0=ALU.mult, op1=ALU.add
            )
            rstd = small.tile([P, TOKEN_TILES, 1], F32, tag="rstd")
            nc.gpsimd.tensor_tensor(out=rstd[:], in0=var_eps[:], in1=minus_half[:], op=ALU.pow)
            return rstd

        def centre_times_gain(dest, src, minus_mean, gain):
            nc.vector.scalar_tensor_tensor(
                out=dest[:], in0=src[:], scalar=minus_mean, in1=gain[:], op0=ALU.add, op1=ALU.mult
            )

        ident = consts.tile([P, P], BF16)
        make_identity(nc, ident[:])
        minus_half = consts.tile([P, TOKEN_TILES, 1], F32)
        nc.vector.memset(minus_half[:], -0.5)

        norm_rows, norm_first = load_as_rows("norm", (bo, ln2_g, ln2_b, fln_g, fln_b))
        h_sb = consts.tile([P, TOKEN_TILES, D], BF16)
        nc.sync.dma_start(
            out=h_sb[:], in_=h_attn.flatten_outer_dims().rearrange("(m p) d -> p m d", p=P)
        )
        x_sb = consts.tile([P, TOKEN_TILES, D], BF16)
        nc.sync.dma_start(out=x_sb[:], in_=x.flatten_outer_dims().rearrange("(m p) d -> p m d", p=P))
        for u in range(PASSES):
            load(u)
        bias_rows, bias_first = load_as_rows("bias", (b1, b2))
        for u in range(PASSES, RAW_BUFS):
            load(u)

        bo_all = spread("bo", norm_rows, norm_first[0], D, nc.vector.tensor_copy)
        x_plus_bo = []
        for m in range(TOKEN_TILES):
            sum_row = rows.tile([P, D], F32, tag="row")
            nc.vector.tensor_tensor(out=sum_row[:], in0=x_sb[:, m, :], in1=bo_all[:], op=ALU.add)
            x_plus_bo.append(sum_row)
        h_grouped = [flip_tokens(h_sb[:, m, :]) for m in range(TOKEN_TILES)]
        h_q = [quantise_tokens("h%d" % m, h_grouped[m]) for m in range(TOKEN_TILES)]
        ln2_g_all = spread("ln2_g", norm_rows, norm_first[1], D, nc.scalar.copy)
        regroup(0, TOGETHER_COLS)
        ln2_b_all = spread("ln2_b", norm_rows, norm_first[2], D, nc.scalar.copy)
        quantise(0)
        multiply(0, h_q)
        regroup(1, TOGETHER_COLS)
        quantise(1)
        multiply(1, h_q)

        regroup(2, 0)
        half_sums, minus_mean, sum_sq = new_statistics()
        r = []
        for m in range(TOKEN_TILES):
            r_row = rows.tile([P, D], F32, tag="row")
            for n in range(UNIT_BANKS):
                cols = slice(n * BANK, (n + 1) * BANK)
                nc.vector.scalar_tensor_tensor(
                    out=r_row[:, cols],
                    in0=banks[(0, m, n)][:],
                    scalar=1.0,
                    in1=x_plus_bo[m][:, cols],
                    op0=ALU.mult,
                    op1=ALU.add,
                    accum_out=half_sums[:, m, n : n + 1],
                )
            measure(m, r_row, half_sums, minus_mean, sum_sq)
            r.append(r_row)
        rstd = rstd_of(sum_sq)
        fln_g_all = spread("fln_g", norm_rows, norm_first[3], D, nc.scalar.copy)
        fln_b_all = spread("fln_b", norm_rows, norm_first[4], D, nc.scalar.copy)
        for m in range(TOKEN_TILES):
            centre_times_gain(r[m], r[m], minus_mean[:, m, :], ln2_g_all)
        quantise(2)
        b1_all = spread("b1", bias_rows, bias_first[0], F, nc.scalar.copy)
        half_sums, minus_mean, sum_sq = new_statistics()
        for m in range(TOKEN_TILES):
            for n in range(UNIT_BANKS):
                cols = slice(n * BANK, (n + 1) * BANK)
                nc.vector.scalar_tensor_tensor(
                    out=r[m][:, cols],
                    in0=r[m][:, cols],
                    scalar=rstd[:, m, :],
                    in1=ln2_b_all[:, cols],
                    op0=ALU.mult,
                    op1=ALU.add,
                    accum_out=half_sums[:, m, n : n + 1],
                )
            nc.sync.dma_start(out=r_out[m * P : (m + 1) * P, :], in_=r[m][:])
            measure(m, r[m], half_sums, minus_mean, sum_sq)
        rstd = rstd_of(sum_sq)
        centred = []
        for m in range(TOKEN_TILES):
            centred_row = rows.tile([P, D], F32, tag="row")
            centre_times_gain(centred_row, r[m], minus_mean[:, m, :], fln_g_all)
            centred.append(centred_row)
        regroup(3, 0)
        h2_grouped = []
        for m in range(TOKEN_TILES):
            h2 = acts.tile([P, D], BF16, tag="h2")
            nc.vector.scalar_tensor_tensor(
                out=h2[:],
                in0=centred[m][:],
                scalar=rstd[:, m, :],
                in1=fln_b_all[:],
                op0=ALU.mult,
                op1=ALU.add,
            )
            h2_grouped.append(flip_tokens(h2))
        b2_all = spread("b2", bias_rows, bias_first[1], F, nc.scalar.copy)
        regroup(4, UNIT_COLS)
        regroup(5, UNIT_COLS)
        quantise(3)
        h2_q = [quantise_tokens("h2_%d" % m, h2_grouped[m]) for m in range(TOKEN_TILES)]

        def finish(chunk, m):
            w, first_col, g = units[chunk * PASSES]
            out, bias = (out_1, b1_all) if w is W1 else (out_2, b2_all)
            staged = staged_pool.tile([P, UNIT_COLS], F32, tag="staged")
            for n in range(UNIT_BANKS):
                nc.vector.tensor_tensor(
                    out=staged[:, n * BANK : (n + 1) * BANK],
                    in0=banks[(chunk, m, n)][:],
                    in1=bias[:, first_col + n * BANK : first_col + (n + 1) * BANK],
                    op=ALU.add,
                )
            nc.sync.dma_start(
                out=out.flatten_outer_dims()[m * P : (m + 1) * P, first_col : first_col + UNIT_COLS],
                in_=staged[:],
            )

        for u in range(PASSES, 2 * PASSES):
            multiply(u, h2_q)
        for u in range(3 * PASSES, len(units) + LAG):
            quantise(u - LAG)
            multiply(u - LAG, h2_q)
            if u < len(units):
                regroup(u, STEADY_COLS)
            finish((u - LAG - PASSES) // PASSES, u % TOKEN_TILES)
        for m in range(TOKEN_TILES):
            finish(last_chunk, m)
